import numpy as np
import ml_dtypes


def mxq(x, axis, fmt="e4m3"):
    dtype, down = {"e4m3": (ml_dtypes.float8_e4m3fn, 7), "e5m2": (ml_dtypes.float8_e5m2, 14)}[fmt]
    v = np.moveaxis(np.asarray(x, np.float32).astype(ml_dtypes.bfloat16).astype(np.float64), axis, -1)
    blocks = v.reshape(v.shape[:-1] + (-1, 32))
    amax = np.abs(blocks).max(-1, keepdims=True)
    byte = np.maximum(np.where(amax > 0, np.frexp(amax)[1] - 1 + 127, 0) - down, 1)
    scale = np.exp2(byte - 127.0)
    codes = (blocks / scale).astype(np.float32).astype(dtype).astype(np.float64)
    return np.moveaxis((codes * scale).reshape(v.shape), -1, axis)


WIDE = False


def mx_kscale(k):
    if not WIDE:
        return np.ones(k)
    levels = np.array([10, -10, 5, -5, 0])
    a = np.random.permutation(np.resize(levels, k // 512 * 4)).reshape(k // 512, 4)
    idx = np.arange(k)
    return np.exp2(a[idx // 512, idx % 128 // 32])


BF16 = ml_dtypes.bfloat16


def bf(x):
    return np.asarray(x, np.float32).astype(BF16)


def f64(x):
    return np.asarray(x).astype(np.float64)


B, DIM = 2048, 1024


def setup_inputs():
    s = mx_kscale(DIM)
    p = np.random.standard_normal((B, DIM)) / s
    q = np.random.standard_normal((B, DIM)) * s
    A = np.random.standard_normal((DIM, DIM)) * 0.7 / np.sqrt(DIM) / s[:, None] / s[None, :]
    return {"pq": bf(np.concatenate([p, q], axis=1)), "A": bf(A)}


def reference(pq, A):
    pq, A = f64(pq), f64(A)
    S = A + A.T
    p = pq[..., :DIM]
    q = pq[..., DIM:]
    pterm = mxq(q, 1, "e4m3") @ mxq(S, 1, "e4m3").T
    return np.concatenate([p + pterm, q], axis=-1)

@@ -1,0 +1,161 @@
+from contextlib import ExitStack
+
+import concourse.mybir as mybir
+from concourse.masks import make_identity
+
+FLOPS = 2 * 2048 * 1024 * 1024
+
+F32 = mybir.dt.float32
+BF16 = mybir.dt.bfloat16
+U32 = mybir.dt.uint32
+U8 = mybir.dt.uint8
+FP8X4 = mybir.dt.float8_e4m3fn_x4
+ADD = mybir.AluOpType.add
+
+P = 128
+B = 2048
+DIM = 1024
+T = B // P
+CHUNK_T = 4
+PAIRS = T // 2
+O_BUFS = 6
+
+
+def tile_linear_sub_kernel(tc, pq, A, out):
+    nc = tc.nc
+    with ExitStack() as ctx:
+        keep = ctx.enter_context(tc.tile_pool(name="keep", bufs=1))
+        qpool = ctx.enter_context(tc.tile_pool(name="qpool", bufs=3))
+        opool = ctx.enter_context(tc.tile_pool(name="opool", bufs=O_BUFS))
+        tpsum = ctx.enter_context(tc.psum_pool(name="tpsum", bufs=2))
+        apsum = ctx.enter_context(tc.psum_pool(name="apsum", bufs=4))
+
+        pq_v = pq.rearrange("(p t) c -> p t c", t=T)
+        out_v = out.rearrange("(p t) c -> p t c", t=T)
+        a_v = A.rearrange("(g u p e) c -> g p u (e c)", g=2, u=2, p=P, e=2)
+
+        a_sb = []
+        for g in range(2):
+            a_t = keep.tile([P, 4 * DIM], BF16, name="a_sb%d" % g)
+            nc.sync.dma_start(out=a_t[:].rearrange("p (u x) -> p u x", u=2), in_=a_v[g])
+            a_sb.append(a_t)
+        pq_sb = []
+        for i in range(T // CHUNK_T):
+            pq_t = keep.tile([P, CHUNK_T * 2 * DIM], BF16, name="pq_sb%d" % i)
+            nc.sync.dma_start(
+                out=pq_t[:].rearrange("p (t c) -> p t c", t=CHUNK_T),
+                in_=pq_v[:, CHUNK_T * i : CHUNK_T * (i + 1), :],
+            )
+            pq_sb.append(pq_t)
+
+        ident = keep.tile([P, P], F32, name="ident")
+        make_identity(nc, ident[:])
+
+        s_codes = []
+        s_scl = []
+        for g in range(2):
+            s_grp = keep.tile([P, 4 * DIM], BF16, name="s_grp%d" % g, align_bytes=64)
+            s_c = keep.tile([P, DIM], U32, name="s_codes%d" % g, align_bytes=64)
+            s_s = keep.tile([P, DIM], U8, name="s_scl%d" % g, align_bytes=64)
+            for jc in range(4):
+                at_ps = tpsum.tile([P, 512], F32, name="at_ps", tag="at")
+                a_w = a_sb[jc // 2][:].bitcast(F32)
+                for ec in range(2):
+                    for u in range(2):
+                        w0 = (jc % 2) * 1024 + ec * 512 + 128 * (2 * g + u)
+                        pos = ec * 2 + u
+                        nc.tensor.transpose(
+                            out=at_ps[:, 128 * pos : 128 * pos + 128],
+                            in_=a_w[:, w0 : w0 + 128],
+                            identity=ident[:],
+                        )
+                nc.vector.tensor_tensor(
+                    out=s_grp[:, 1024 * jc : 1024 * jc + 1024].rearrange(
+                        "p (pc ec u e) -> p pc ec u e", pc=P, ec=2, u=2, e=2
+                    ),
+                    in0=at_ps[:].bitcast(BF16).rearrange(
+                        "p (ec u pc e) -> p pc ec u e", ec=2, u=2, pc=P, e=2
+                    ),
+                    in1=a_sb[g][:]
+                    .rearrange("p (u e c) -> p u e c", u=2, e=2)[:, :, :, 256 * jc : 256 * jc + 256]
+                    .rearrange("p u e (pc ec) -> p pc ec u e", ec=2),
+                    op=ADD,
+                )
+                if jc % 2 == 1:
+                    h = jc // 2
+                    nc.vector.quantize_mx(
+                        out=s_c[:, 512 * h : 512 * h + 512].bitcast(FP8X4),
+                        scales=s_s[:, 512 * h : 512 * h + 512],
+                        in_=s_grp[:, 2048 * h : 2048 * h + 2048],
+                    )
+            s_codes.append(s_c)
+            s_scl.append(s_s)
+
+        state = {}
+
+        def prep(k):
+            pq_t = pq_sb[k // 2]
+            pq_w = pq_t[:].bitcast(F32)
+            o_sb = opool.tile([P, 2 * 2 * DIM], F32, name="o_sb")
+            q_grp = qpool.tile([P, 2048], BF16, name="q_grp", align_bytes=64)
+            q_c = qpool.tile([P, 512], U32, name="q_codes", align_bytes=64)
+            q_s = qpool.tile([P, 512], U8, name="q_scl", align_bytes=64)
+            q_grp_w = q_grp[:].bitcast(F32)
+            for tt in range(2):
+                t4 = 2 * (k % 2) + tt
+                qt_ps = tpsum.tile([P, 512], F32, name="qt_ps", tag="qt")
+                for jw in range(4):
+                    w0 = t4 * 1024 + 512 + 128 * jw
+                    nc.tensor.transpose(
+                        out=qt_ps[:, 128 * jw : 128 * jw + 128],
+                        in_=pq_w[:, w0 : w0 + 128],
+                        identity=ident[:],
+                    )
+                nc.scalar.copy(
+                    out=q_grp_w[:, 512 * tt : 512 * tt + 512].rearrange(
+                        "p (g b u) -> p g b u", g=2, b=P, u=2
+                    ),
+                    in_=qt_ps[:].rearrange("p (g u b) -> p g b u", g=2, u=2, b=P),
+                )
+            t0 = 2 * (k % 2)
+            nc.scalar.copy(
+                out=o_sb[:].rearrange("p (t c) -> p t c", t=2)[:, :, DIM : 2 * DIM],
+                in_=pq_t[:].rearrange("p (t c) -> p t c", t=CHUNK_T)[:, t0 : t0 + 2, DIM : 2 * DIM],
+            )
+            nc.vector.quantize_mx(out=q_c[:].bitcast(FP8X4), scales=q_s[:], in_=q_grp[:])
+            state[k] = (o_sb, q_c, q_s)
+
+        def main(k):
+            pq_t = pq_sb[k // 2]
+            o_sb, q_c, q_s = state[k]
+            for tt in range(2):
+                t4 = 2 * (k % 2) + tt
+                for h in range(2):
+                    acc = apsum.tile([P, 512], F32, name="acc")
+                    for g in range(2):
+                        c0 = 256 * tt + 128 * g
+                        nc.tensor.matmul_mx(
+                            out=acc[:],
+                            lhsT=q_c[:, c0 : c0 + 128].bitcast(FP8X4),
+                            lhsT_scale=q_s[:, c0 : c0 + 128],
+                            rhs=s_codes[g][:, 512 * h : 512 * h + 512].bitcast(FP8X4),
+                            rhs_scale=s_scl[g][:, 512 * h : 512 * h + 512],
+                            start=(g == 0),
+                            stop=(g == 1),
+                        )
+                    nc.vector.tensor_tensor(
+                        out=o_sb[:, 2048 * tt + 512 * h : 2048 * tt + 512 * h + 512],
+                        in0=acc[:],
+                        in1=pq_t[:, 2048 * t4 + 512 * h : 2048 * t4 + 512 * h + 512],
+                        op=ADD,
+                    )
+            nc.sync.dma_start(
+                out=out_v[:, 2 * k : 2 * k + 2, :],
+                in_=o_sb[:].rearrange("p (t c) -> p t c", t=2),
+            )
+
+        prep(0)
+        for k in range(PAIRS):
+            if k + 1 < PAIRS:
+                prep(k + 1)
+            main(k)

@@ -19,6 +19,7 @@ T = B // P
 CHUNK_T = 4
 PAIRS = T // 2
 O_BUFS = 6
+SPLIT_PAIRS = 2
 
 
 def tile_linear_sub_kernel(tc, pq, A, out):
@@ -122,6 +123,11 @@ def tile_linear_sub_kernel(tc, pq, A, out):
                 out=o_sb[:].rearrange("p (t c) -> p t c", t=2)[:, :, DIM : 2 * DIM],
                 in_=pq_t[:].rearrange("p (t c) -> p t c", t=CHUNK_T)[:, t0 : t0 + 2, DIM : 2 * DIM],
             )
+            if k < SPLIT_PAIRS:
+                nc.sync.dma_start(
+                    out=out_v[:, 2 * k : 2 * k + 2, DIM : 2 * DIM],
+                    in_=o_sb[:].rearrange("p (t c) -> p t c", t=2)[:, :, DIM : 2 * DIM],
+                )
             nc.vector.quantize_mx(out=q_c[:].bitcast(FP8X4), scales=q_s[:], in_=q_grp[:])
             state[k] = (o_sb, q_c, q_s)
 
@@ -149,9 +155,10 @@ def tile_linear_sub_kernel(tc, pq, A, out):
                         in1=pq_t[:, 2048 * t4 + 512 * h : 2048 * t4 + 512 * h + 512],
                         op=ADD,
                     )
+            width = DIM if k < SPLIT_PAIRS else 2 * DIM
             nc.sync.dma_start(
-                out=out_v[:, 2 * k : 2 * k + 2, :],
-                in_=o_sb[:].rearrange("p (t c) -> p t c", t=2),
+                out=out_v[:, 2 * k : 2 * k + 2, 0:width],
+                in_=o_sb[:].rearrange("p (t c) -> p t c", t=2)[:, :, 0:width],
             )
 
         prep(0)

@@ -19,7 +19,6 @@ T = B // P
 CHUNK_T = 4
 PAIRS = T // 2
 O_BUFS = 6
-SPLIT_PAIRS = 2
 
 
 def tile_linear_sub_kernel(tc, pq, A, out):
@@ -28,8 +27,9 @@ def tile_linear_sub_kernel(tc, pq, A, out):
         keep = ctx.enter_context(tc.tile_pool(name="keep", bufs=1))
         qpool = ctx.enter_context(tc.tile_pool(name="qpool", bufs=3))
         opool = ctx.enter_context(tc.tile_pool(name="opool", bufs=O_BUFS))
-        tpsum = ctx.enter_context(tc.psum_pool(name="tpsum", bufs=2))
+        tpsum = ctx.enter_context(tc.psum_pool(name="tpsum", bufs=4))
         apsum = ctx.enter_context(tc.psum_pool(name="apsum", bufs=4))
+        ctx.enter_context(tc.manual_schedule())
 
         pq_v = pq.rearrange("(p t) c -> p t c", t=T)
         out_v = out.rearrange("(p t) c -> p t c", t=T)
@@ -52,59 +52,61 @@ def tile_linear_sub_kernel(tc, pq, A, out):
         ident = keep.tile([P, P], F32, name="ident")
         make_identity(nc, ident[:])
 
+        s_grp = []
         s_codes = []
         s_scl = []
         for g in range(2):
-            s_grp = keep.tile([P, 4 * DIM], BF16, name="s_grp%d" % g, align_bytes=64)
-            s_c = keep.tile([P, DIM], U32, name="s_codes%d" % g, align_bytes=64)
-            s_s = keep.tile([P, DIM], U8, name="s_scl%d" % g, align_bytes=64)
-            for jc in range(4):
-                at_ps = tpsum.tile([P, 512], F32, name="at_ps", tag="at")
-                a_w = a_sb[jc // 2][:].bitcast(F32)
-                for ec in range(2):
-                    for u in range(2):
-                        w0 = (jc % 2) * 1024 + ec * 512 + 128 * (2 * g + u)
-                        pos = ec * 2 + u
-                        nc.tensor.transpose(
-                            out=at_ps[:, 128 * pos : 128 * pos + 128],
-                            in_=a_w[:, w0 : w0 + 128],
-                            identity=ident[:],
-                        )
-                nc.vector.tensor_tensor(
-                    out=s_grp[:, 1024 * jc : 1024 * jc + 1024].rearrange(
-                        "p (pc ec u e) -> p pc ec u e", pc=P, ec=2, u=2, e=2
-                    ),
-                    in0=at_ps[:].bitcast(BF16).rearrange(
-                        "p (ec u pc e) -> p pc ec u e", ec=2, u=2, pc=P, e=2
-                    ),
-                    in1=a_sb[g][:]
-                    .rearrange("p (u e c) -> p u e c", u=2, e=2)[:, :, :, 256 * jc : 256 * jc + 256]
-                    .rearrange("p u e (pc ec) -> p pc ec u e", ec=2),
-                    op=ADD,
-                )
-                if jc % 2 == 1:
-                    h = jc // 2
-                    nc.vector.quantize_mx(
-                        out=s_c[:, 512 * h : 512 * h + 512].bitcast(FP8X4),
-                        scales=s_s[:, 512 * h : 512 * h + 512],
-                        in_=s_grp[:, 2048 * h : 2048 * h + 2048],
-                    )
-            s_codes.append(s_c)
-            s_scl.append(s_s)
+            s_grp.append(keep.tile([P, 4 * DIM], BF16, name="s_grp%d" % g, align_bytes=64))
+            s_codes.append(keep.tile([P, DIM], U32, name="s_codes%d" % g, align_bytes=64))
+            s_scl.append(keep.tile([P, DIM], U8, name="s_scl%d" % g, align_bytes=64))
 
+        at_tiles = {}
+        qt_tiles = {}
         state = {}
 
-        def prep(k):
-            pq_t = pq_sb[k // 2]
-            pq_w = pq_t[:].bitcast(F32)
-            o_sb = opool.tile([P, 2 * 2 * DIM], F32, name="o_sb")
-            q_grp = qpool.tile([P, 2048], BF16, name="q_grp", align_bytes=64)
-            q_c = qpool.tile([P, 512], U32, name="q_codes", align_bytes=64)
-            q_s = qpool.tile([P, 512], U8, name="q_scl", align_bytes=64)
-            q_grp_w = q_grp[:].bitcast(F32)
+        def a_transposes(n):
+            g, jc = divmod(n, 4)
+            at_ps = tpsum.tile([P, 512], F32, name="at_ps", tag="tp")
+            a_w = a_sb[jc // 2][:].bitcast(F32)
+            for ec in range(2):
+                for u in range(2):
+                    w0 = (jc % 2) * 1024 + ec * 512 + 128 * (2 * g + u)
+                    pos = ec * 2 + u
+                    nc.tensor.transpose(
+                        out=at_ps[:, 128 * pos : 128 * pos + 128],
+                        in_=a_w[:, w0 : w0 + 128],
+                        identity=ident[:],
+                    )
+            at_tiles[n] = at_ps
+
+        def s_add(n):
+            g, jc = divmod(n, 4)
+            nc.vector.tensor_tensor(
+                out=s_grp[g][:, 1024 * jc : 1024 * jc + 1024].rearrange(
+                    "p (pc ec u e) -> p pc ec u e", pc=P, ec=2, u=2, e=2
+                ),
+                in0=at_tiles[n][:].bitcast(BF16).rearrange(
+                    "p (ec u pc e) -> p pc ec u e", ec=2, u=2, pc=P, e=2
+                ),
+                in1=a_sb[g][:]
+                .rearrange("p (u e c) -> p u e c", u=2, e=2)[:, :, :, 256 * jc : 256 * jc + 256]
+                .rearrange("p u e (pc ec) -> p pc ec u e", ec=2),
+                op=ADD,
+            )
+
+        def s_quantise(g, h):
+            nc.vector.quantize_mx(
+                out=s_codes[g][:, 512 * h : 512 * h + 512].bitcast(FP8X4),
+                scales=s_scl[g][:, 512 * h : 512 * h + 512],
+                in_=s_grp[g][:, 2048 * h : 2048 * h + 2048],
+            )
+
+        def q_transposes(k):
+            pq_w = pq_sb[k // 2][:].bitcast(F32)
+            banks = []
             for tt in range(2):
                 t4 = 2 * (k % 2) + tt
-                qt_ps = tpsum.tile([P, 512], F32, name="qt_ps", tag="qt")
+                qt_ps = tpsum.tile([P, 512], F32, name="qt_ps", tag="tp")
                 for jw in range(4):
                     w0 = t4 * 1024 + 512 + 128 * jw
                     nc.tensor.transpose(
@@ -112,30 +114,38 @@ def tile_linear_sub_kernel(tc, pq, A, out):
                         in_=pq_w[:, w0 : w0 + 128],
                         identity=ident[:],
                     )
+                banks.append(qt_ps)
+            qt_tiles[k] = banks
+
+        def q_copies(k):
+            pq_t = pq_sb[k // 2]
+            o_sb = opool.tile([P, 2 * 2 * DIM], F32, name="o_sb")
+            q_grp = qpool.tile([P, 2048], BF16, name="q_grp", align_bytes=64)
+            q_grp_w = q_grp[:].bitcast(F32)
+            for tt in range(2):
                 nc.scalar.copy(
                     out=q_grp_w[:, 512 * tt : 512 * tt + 512].rearrange(
                         "p (g b u) -> p g b u", g=2, b=P, u=2
                     ),
-                    in_=qt_ps[:].rearrange("p (g u b) -> p g b u", g=2, u=2, b=P),
+                    in_=qt_tiles[k][tt][:].rearrange("p (g u b) -> p g b u", g=2, u=2, b=P),
                 )
             t0 = 2 * (k % 2)
             nc.scalar.copy(
                 out=o_sb[:].rearrange("p (t c) -> p t c", t=2)[:, :, DIM : 2 * DIM],
                 in_=pq_t[:].rearrange("p (t c) -> p t c", t=CHUNK_T)[:, t0 : t0 + 2, DIM : 2 * DIM],
             )
-            if k < SPLIT_PAIRS:
-                nc.sync.dma_start(
-                    out=out_v[:, 2 * k : 2 * k + 2, DIM : 2 * DIM],
-                    in_=o_sb[:].rearrange("p (t c) -> p t c", t=2)[:, :, DIM : 2 * DIM],
-                )
-            nc.vector.quantize_mx(out=q_c[:].bitcast(FP8X4), scales=q_s[:], in_=q_grp[:])
-            state[k] = (o_sb, q_c, q_s)
+            state[k] = [o_sb, q_grp]
 
-        def main(k):
-            pq_t = pq_sb[k // 2]
-            o_sb, q_c, q_s = state[k]
+        def q_quantise(k):
+            q_c = qpool.tile([P, 512], U32, name="q_codes", align_bytes=64)
+            q_s = qpool.tile([P, 512], U8, name="q_scl", align_bytes=64)
+            nc.vector.quantize_mx(out=q_c[:].bitcast(FP8X4), scales=q_s[:], in_=state[k][1][:])
+            state[k].extend([q_c, q_s])
+
+        def passes(k):
+            q_c, q_s = state[k][2], state[k][3]
+            accs = []
             for tt in range(2):
-                t4 = 2 * (k % 2) + tt
                 for h in range(2):
                     acc = apsum.tile([P, 512], F32, name="acc")
                     for g in range(2):
@@ -149,20 +159,66 @@ def tile_linear_sub_kernel(tc, pq, A, out):
                             start=(g == 0),
                             stop=(g == 1),
                         )
-                    nc.vector.tensor_tensor(
-                        out=o_sb[:, 2048 * tt + 512 * h : 2048 * tt + 512 * h + 512],
-                        in0=acc[:],
-                        in1=pq_t[:, 2048 * t4 + 512 * h : 2048 * t4 + 512 * h + 512],
-                        op=ADD,
-                    )
-            width = DIM if k < SPLIT_PAIRS else 2 * DIM
+                    accs.append(acc)
+            state[k].append(accs)
+
+        def p_adds(k, tt):
+            pq_t = pq_sb[k // 2]
+            o_sb = state[k][0]
+            t4 = 2 * (k % 2) + tt
+            for h in range(2):
+                nc.vector.tensor_tensor(
+                    out=o_sb[:, 2048 * tt + 512 * h : 2048 * tt + 512 * h + 512],
+                    in0=state[k][4][2 * tt + h][:],
+                    in1=pq_t[:, 2048 * t4 + 512 * h : 2048 * t4 + 512 * h + 512],
+                    op=ADD,
+                )
+
+        def store(k, tt0, tt1):
             nc.sync.dma_start(
-                out=out_v[:, 2 * k : 2 * k + 2, 0:width],
-                in_=o_sb[:].rearrange("p (t c) -> p t c", t=2)[:, :, 0:width],
+                out=out_v[:, 2 * k + tt0 : 2 * k + tt1, :],
+                in_=state[k][0][:].rearrange("p (t c) -> p t c", t=2)[:, tt0:tt1, :],
             )
 
-        prep(0)
-        for k in range(PAIRS):
-            if k + 1 < PAIRS:
-                prep(k + 1)
-            main(k)
+        for n in range(4):
+            a_transposes(n)
+        s_add(0)
+        s_add(1)
+        a_transposes(4)
+        a_transposes(5)
+        s_add(2)
+        s_quantise(0, 0)
+        s_add(3)
+        q_transposes(0)
+        q_copies(0)
+        s_add(4)
+        s_quantise(0, 1)
+        s_add(5)
+        a_transposes(6)
+        a_transposes(7)
+        s_add(6)
+        s_quantise(1, 0)
+        s_add(7)
+        q_transposes(1)
+        q_copies(1)
+        q_transposes(2)
+        q_copies(2)
+        q_quantise(0)
+        s_quantise(1, 1)
+        passes(0)
+        p_adds(0, 0)
+        store(0, 0, 1)
+        q_quantise(1)
+        p_adds(0, 1)
+        store(0, 1, 2)
+        q_quantise(2)
+        for k in range(1, PAIRS):
+            if k + 2 < PAIRS:
+                q_transposes(k + 2)
+                q_copies(k + 2)
+            passes(k)
+            p_adds(k, 0)
+            p_adds(k, 1)
+            store(k, 0, 2)
+            if k + 2 < PAIRS:
+                q_quantise(k + 2)

from contextlib import ExitStack

import concourse.mybir as mybir
from concourse.masks import make_identity

FLOPS = 2 * 2048 * 1024 * 1024

F32 = mybir.dt.float32
BF16 = mybir.dt.bfloat16
U32 = mybir.dt.uint32
U8 = mybir.dt.uint8
FP8X4 = mybir.dt.float8_e4m3fn_x4
ADD = mybir.AluOpType.add

P = 128
B = 2048
DIM = 1024
T = B // P
CHUNK_T = 4
PAIRS = T // 2
O_BUFS = 6


def tile_linear_sub_kernel(tc, pq, A, out):
    nc = tc.nc
    with ExitStack() as ctx:
        keep = ctx.enter_context(tc.tile_pool(name="keep", bufs=1))
        qpool = ctx.enter_context(tc.tile_pool(name="qpool", bufs=3))
        opool = ctx.enter_context(tc.tile_pool(name="opool", bufs=O_BUFS))
        tpsum = ctx.enter_context(tc.psum_pool(name="tpsum", bufs=4))
        apsum = ctx.enter_context(tc.psum_pool(name="apsum", bufs=4))
        ctx.enter_context(tc.manual_schedule())

        pq_v = pq.rearrange("(p t) c -> p t c", t=T)
        out_v = out.rearrange("(p t) c -> p t c", t=T)
        a_v = A.rearrange("(g u p e) c -> g p u (e c)", g=2, u=2, p=P, e=2)

        a_sb = []
        for g in range(2):
            a_t = keep.tile([P, 4 * DIM], BF16, name="a_sb%d" % g)
            nc.sync.dma_start(out=a_t[:].rearrange("p (u x) -> p u x", u=2), in_=a_v[g])
            a_sb.append(a_t)
        pq_sb = []
        for i in range(T // CHUNK_T):
            pq_t = keep.tile([P, CHUNK_T * 2 * DIM], BF16, name="pq_sb%d" % i)
            nc.sync.dma_start(
                out=pq_t[:].rearrange("p (t c) -> p t c", t=CHUNK_T),
                in_=pq_v[:, CHUNK_T * i : CHUNK_T * (i + 1), :],
            )
            pq_sb.append(pq_t)

        ident = keep.tile([P, P], F32, name="ident")
        make_identity(nc, ident[:])

        s_grp = []
        s_codes = []
        s_scl = []
        for g in range(2):
            s_grp.append(keep.tile([P, 4 * DIM], BF16, name="s_grp%d" % g, align_bytes=64))
            s_codes.append(keep.tile([P, DIM], U32, name="s_codes%d" % g, align_bytes=64))
            s_scl.append(keep.tile([P, DIM], U8, name="s_scl%d" % g, align_bytes=64))

        at_tiles = {}
        qt_tiles = {}
        state = {}

        def a_transposes(n):
            g, jc = divmod(n, 4)
            at_ps = tpsum.tile([P, 512], F32, name="at_ps", tag="tp")
            a_w = a_sb[jc // 2][:].bitcast(F32)
            for ec in range(2):
                for u in range(2):
                    w0 = (jc % 2) * 1024 + ec * 512 + 128 * (2 * g + u)
                    pos = ec * 2 + u
                    nc.tensor.transpose(
                        out=at_ps[:, 128 * pos : 128 * pos + 128],
                        in_=a_w[:, w0 : w0 + 128],
                        identity=ident[:],
                    )
            at_tiles[n] = at_ps

        def s_add(n):
            g, jc = divmod(n, 4)
            nc.vector.tensor_tensor(
                out=s_grp[g][:, 1024 * jc : 1024 * jc + 1024].rearrange(
                    "p (pc ec u e) -> p pc ec u e", pc=P, ec=2, u=2, e=2
                ),
                in0=at_tiles[n][:].bitcast(BF16).rearrange(
                    "p (ec u pc e) -> p pc ec u e", ec=2, u=2, pc=P, e=2
                ),
                in1=a_sb[g][:]
                .rearrange("p (u e c) -> p u e c", u=2, e=2)[:, :, :, 256 * jc : 256 * jc + 256]
                .rearrange("p u e (pc ec) -> p pc ec u e", ec=2),
                op=ADD,
            )

        def s_quantise(g, h):
            nc.vector.quantize_mx(
                out=s_codes[g][:, 512 * h : 512 * h + 512].bitcast(FP8X4),
                scales=s_scl[g][:, 512 * h : 512 * h + 512],
                in_=s_grp[g][:, 2048 * h : 2048 * h + 2048],
            )

        def q_transposes(k):
            pq_w = pq_sb[k // 2][:].bitcast(F32)
            banks = []
            for tt in range(2):
                t4 = 2 * (k % 2) + tt
                qt_ps = tpsum.tile([P, 512], F32, name="qt_ps", tag="tp")
                for jw in range(4):
                    w0 = t4 * 1024 + 512 + 128 * jw
                    nc.tensor.transpose(
                        out=qt_ps[:, 128 * jw : 128 * jw + 128],
                        in_=pq_w[:, w0 : w0 + 128],
                        identity=ident[:],
                    )
                banks.append(qt_ps)
            qt_tiles[k] = banks

        def q_copies(k):
            pq_t = pq_sb[k // 2]
            o_sb = opool.tile([P, 2 * 2 * DIM], F32, name="o_sb")
            q_grp = qpool.tile([P, 2048], BF16, name="q_grp", align_bytes=64)
            q_grp_w = q_grp[:].bitcast(F32)
            for tt in range(2):
                nc.scalar.copy(
                    out=q_grp_w[:, 512 * tt : 512 * tt + 512].rearrange(
                        "p (g b u) -> p g b u", g=2, b=P, u=2
                    ),
                    in_=qt_tiles[k][tt][:].rearrange("p (g u b) -> p g b u", g=2, u=2, b=P),
                )
            t0 = 2 * (k % 2)
            nc.scalar.copy(
                out=o_sb[:].rearrange("p (t c) -> p t c", t=2)[:, :, DIM : 2 * DIM],
                in_=pq_t[:].rearrange("p (t c) -> p t c", t=CHUNK_T)[:, t0 : t0 + 2, DIM : 2 * DIM],
            )
            state[k] = [o_sb, q_grp]

        def q_quantise(k):
            q_c = qpool.tile([P, 512], U32, name="q_codes", align_bytes=64)
            q_s = qpool.tile([P, 512], U8, name="q_scl", align_bytes=64)
            nc.vector.quantize_mx(out=q_c[:].bitcast(FP8X4), scales=q_s[:], in_=state[k][1][:])
            state[k].extend([q_c, q_s])

        def passes(k):
            q_c, q_s = state[k][2], state[k][3]
            accs = []
            for tt in range(2):
                for h in range(2):
                    acc = apsum.tile([P, 512], F32, name="acc")
                    for g in range(2):
                        c0 = 256 * tt + 128 * g
                        nc.tensor.matmul_mx(
                            out=acc[:],
                            lhsT=q_c[:, c0 : c0 + 128].bitcast(FP8X4),
                            lhsT_scale=q_s[:, c0 : c0 + 128],
                            rhs=s_codes[g][:, 512 * h : 512 * h + 512].bitcast(FP8X4),
                            rhs_scale=s_scl[g][:, 512 * h : 512 * h + 512],
                            start=(g == 0),
                            stop=(g == 1),
                        )
                    accs.append(acc)
            state[k].append(accs)

        def p_adds(k, tt):
            pq_t = pq_sb[k // 2]
            o_sb = state[k][0]
            t4 = 2 * (k % 2) + tt
            for h in range(2):
                nc.vector.tensor_tensor(
                    out=o_sb[:, 2048 * tt + 512 * h : 2048 * tt + 512 * h + 512],
                    in0=state[k][4][2 * tt + h][:],
                    in1=pq_t[:, 2048 * t4 + 512 * h : 2048 * t4 + 512 * h + 512],
                    op=ADD,
                )

        def store(k, tt0, tt1):
            nc.sync.dma_start(
                out=out_v[:, 2 * k + tt0 : 2 * k + tt1, :],
                in_=state[k][0][:].rearrange("p (t c) -> p t c", t=2)[:, tt0:tt1, :],
            )

        for n in range(4):
            a_transposes(n)
        s_add(0)
        s_add(1)
        a_transposes(4)
        a_transposes(5)
        s_add(2)
        s_quantise(0, 0)
        s_add(3)
        q_transposes(0)
        q_copies(0)
        s_add(4)
        s_quantise(0, 1)
        s_add(5)
        a_transposes(6)
        a_transposes(7)
        s_add(6)
        s_quantise(1, 0)
        s_add(7)
        q_transposes(1)
        q_copies(1)
        q_transposes(2)
        q_copies(2)
        q_quantise(0)
        s_quantise(1, 1)
        passes(0)
        p_adds(0, 0)
        store(0, 0, 1)
        q_quantise(1)
        p_adds(0, 1)
        store(0, 1, 2)
        q_quantise(2)
        for k in range(1, PAIRS):
            if k + 2 < PAIRS:
                q_transposes(k + 2)
                q_copies(k + 2)
            passes(k)
            p_adds(k, 0)
            p_adds(k, 1)
            store(k, 0, 2)
            if k + 2 < PAIRS:
                q_quantise(k + 2)
